import numpy as np
import ml_dtypes

BF16 = ml_dtypes.bfloat16


def bf(x):
    return np.asarray(x, np.float32).astype(BF16)


def f32(x):
    return np.asarray(x, np.float32)


def f64(x):
    return np.asarray(x).astype(np.float64)


def striped(idx):
    return np.tile(idx.reshape(-1, 16).T, (8, 1))


C, S, N = 256, 256, 128


def setup_inputs():
    return {
        "x": f32(np.random.standard_normal((C, S))),
        "attr": f32(np.random.standard_normal((1, N))),
        "wa": f32(0.5 * np.random.standard_normal((C, 1))),
        "ba": f32(0.1 * np.random.standard_normal((C, 1))),
        "w1": bf(np.random.standard_normal((C, C)) / np.sqrt(C)),
        "b1": f32(0.1 * np.random.standard_normal((C, 1))),
        "offs": striped(np.random.permutation(np.tile(np.arange(S), 2))[:N]),
    }


def reference(x, attr, wa, ba, w1, b1, offs):
    idx = offs[:16].T.reshape(-1)
    attract = f64(wa) * f64(attr) + f64(ba)
    u = f64(x)[:, idx] + attract
    return np.maximum(f64(w1).T @ u + f64(b1), 0.0)

@@ -1,0 +1,65 @@
+import concourse.mybir as mybir
+
+F32 = mybir.dt.float32
+BF16 = mybir.dt.bfloat16
+U16 = mybir.dt.uint16
+ADD = mybir.AluOpType.add
+MULT = mybir.AluOpType.mult
+MAX = mybir.AluOpType.max
+
+P = 128
+C = 256
+S = 256
+N = 128
+BLOCKS = C // P
+
+FLOPS = 2 * C * C * N
+
+
+def tile_topicpropagationmodel_kernel(tc, x, attr, wa, ba, w1, b1, offs, out):
+    nc = tc.nc
+    with tc.tile_pool(name="held", bufs=1) as held, tc.psum_pool(name="banks", bufs=1) as banks:
+        offsets = held.tile([P, N // 16], U16, name="offsets")
+        nc.sync.dma_start(offsets[:], offs)
+        nodes = []
+        for k in range(BLOCKS):
+            nodes_k = held.tile([P, S], F32, name=f"nodes{k}")
+            nc.sync.dma_start(nodes_k[:], x[k * P : (k + 1) * P, :])
+            nodes.append(nodes_k)
+        scores = held.tile([P, N], F32, name="scores")
+        nc.scalar.dma_start(scores[:], attr.broadcast_to([P, N]))
+        wa_cols = held.tile([P, BLOCKS], F32, name="wa_cols")
+        ba_cols = held.tile([P, BLOCKS], F32, name="ba_cols")
+        b1_cols = held.tile([P, BLOCKS], F32, name="b1_cols")
+        with nc.allow_non_contiguous_dma(reason="one float32 to a partition, 256 in all"):
+            nc.scalar.dma_start(wa_cols[:], wa.rearrange("(k p) o -> p (k o)", p=P))
+            nc.scalar.dma_start(ba_cols[:], ba.rearrange("(k p) o -> p (k o)", p=P))
+            nc.scalar.dma_start(b1_cols[:], b1.rearrange("(k p) o -> p (k o)", p=P))
+        weights = held.tile([P, BLOCKS, C], BF16, name="weights")
+        nc.gpsimd.dma_start(weights[:], w1.rearrange("(k p) m -> p k m", p=P))
+
+        hidden_in = []
+        for k in range(BLOCKS):
+            attract = held.tile([P, N], F32, name=f"attract{k}")
+            nc.vector.tensor_scalar(
+                attract[:], scores[:], wa_cols[:, k : k + 1], ba_cols[:, k : k + 1], MULT, ADD
+            )
+            u_f32 = held.tile([P, N], F32, name=f"u_f32_{k}")
+            nc.vector.tensor_tensor(u_f32[:], nodes[k][:].indirect(offsets[:]), attract[:], ADD)
+            u_bf16 = held.tile([P, N], BF16, name=f"u_bf16_{k}")
+            nc.vector.tensor_copy(u_bf16[:], u_f32[:])
+            hidden_in.append(u_bf16)
+
+        for m in range(BLOCKS):
+            product = banks.tile([P, N], F32, name=f"product{m}")
+            for k in range(BLOCKS):
+                nc.tensor.matmul(
+                    product[:],
+                    weights[:, k, m * P : (m + 1) * P],
+                    hidden_in[k][:],
+                    start=(k == 0),
+                    stop=(k == BLOCKS - 1),
+                )
+            result = held.tile([P, N], F32, name=f"result{m}")
+            nc.vector.tensor_scalar(result[:], product[:], b1_cols[:, m : m + 1], 0.0, ADD, MAX)
+            nc.sync.dma_start(out[m * P : (m + 1) * P, :], result[:])

@@ -34,9 +34,10 @@ def tile_topicpropagationmodel_kernel(tc, x, attr, wa, ba, w1, b1, offs, out):
         with nc.allow_non_contiguous_dma(reason="one float32 to a partition, 256 in all"):
             nc.scalar.dma_start(wa_cols[:], wa.rearrange("(k p) o -> p (k o)", p=P))
             nc.scalar.dma_start(ba_cols[:], ba.rearrange("(k p) o -> p (k o)", p=P))
-            nc.scalar.dma_start(b1_cols[:], b1.rearrange("(k p) o -> p (k o)", p=P))
         weights = held.tile([P, BLOCKS, C], BF16, name="weights")
-        nc.gpsimd.dma_start(weights[:], w1.rearrange("(k p) m -> p k m", p=P))
+        nc.scalar.dma_start(weights[:], w1.rearrange("(k p) m -> p k m", p=P))
+        with nc.allow_non_contiguous_dma(reason="one float32 to a partition, 256 in all"):
+            nc.sync.dma_start(b1_cols[:], b1.rearrange("(k p) o -> p (k o)", p=P))
 
         hidden_in = []
         for k in range(BLOCKS):

@@ -39,28 +39,32 @@ def tile_topicpropagationmodel_kernel(tc, x, attr, wa, ba, w1, b1, offs, out):
         with nc.allow_non_contiguous_dma(reason="one float32 to a partition, 256 in all"):
             nc.sync.dma_start(b1_cols[:], b1.rearrange("(k p) o -> p (k o)", p=P))
 
-        hidden_in = []
+        attract = []
         for k in range(BLOCKS):
-            attract = held.tile([P, N], F32, name=f"attract{k}")
+            attract_k = held.tile([P, N], F32, name=f"attract{k}")
             nc.vector.tensor_scalar(
-                attract[:], scores[:], wa_cols[:, k : k + 1], ba_cols[:, k : k + 1], MULT, ADD
+                attract_k[:], scores[:], wa_cols[:, k : k + 1], ba_cols[:, k : k + 1], MULT, ADD
             )
+            attract.append(attract_k)
+
+        product = [banks.tile([P, N], F32, name=f"product{m}") for m in range(BLOCKS)]
+
+        for k in range(BLOCKS):
             u_f32 = held.tile([P, N], F32, name=f"u_f32_{k}")
-            nc.vector.tensor_tensor(u_f32[:], nodes[k][:].indirect(offsets[:]), attract[:], ADD)
+            nc.vector.tensor_tensor(u_f32[:], nodes[k][:].indirect(offsets[:]), attract[k][:], ADD)
             u_bf16 = held.tile([P, N], BF16, name=f"u_bf16_{k}")
             nc.vector.tensor_copy(u_bf16[:], u_f32[:])
-            hidden_in.append(u_bf16)
-
-        for m in range(BLOCKS):
-            product = banks.tile([P, N], F32, name=f"product{m}")
-            for k in range(BLOCKS):
+            for m in range(BLOCKS):
                 nc.tensor.matmul(
-                    product[:],
+                    product[m][:],
                     weights[:, k, m * P : (m + 1) * P],
-                    hidden_in[k][:],
+                    u_bf16[:],
                     start=(k == 0),
                     stop=(k == BLOCKS - 1),
                 )
+
+        store_queues = [nc.sync, nc.scalar]
+        for m in range(BLOCKS):
             result = held.tile([P, N], F32, name=f"result{m}")
-            nc.vector.tensor_scalar(result[:], product[:], b1_cols[:, m : m + 1], 0.0, ADD, MAX)
-            nc.sync.dma_start(out[m * P : (m + 1) * P, :], result[:])
+            nc.vector.tensor_scalar(result[:], product[m][:], b1_cols[:, m : m + 1], 0.0, ADD, MAX)
+            store_queues[m].dma_start(out[m * P : (m + 1) * P, :], result[:])

@@ -63,8 +63,7 @@ def tile_topicpropagationmodel_kernel(tc, x, attr, wa, ba, w1, b1, offs, out):
                     stop=(k == BLOCKS - 1),
                 )
 
-        store_queues = [nc.sync, nc.scalar]
         for m in range(BLOCKS):
             result = held.tile([P, N], F32, name=f"result{m}")
             nc.vector.tensor_scalar(result[:], product[m][:], b1_cols[:, m : m + 1], 0.0, ADD, MAX)
-            store_queues[m].dma_start(out[m * P : (m + 1) * P, :], result[:])
+            nc.sync.dma_start(out[m * P : (m + 1) * P, :], result[:])

@@ -20,24 +20,23 @@ def tile_topicpropagationmodel_kernel(tc, x, attr, wa, ba, w1, b1, offs, out):
     nc = tc.nc
     with tc.tile_pool(name="held", bufs=1) as held, tc.psum_pool(name="banks", bufs=1) as banks:
         offsets = held.tile([P, N // 16], U16, name="offsets")
-        nc.sync.dma_start(offsets[:], offs)
-        nodes = []
-        for k in range(BLOCKS):
-            nodes_k = held.tile([P, S], F32, name=f"nodes{k}")
-            nc.sync.dma_start(nodes_k[:], x[k * P : (k + 1) * P, :])
-            nodes.append(nodes_k)
+        nodes = [held.tile([P, S], F32, name=f"nodes{k}") for k in range(BLOCKS)]
         scores = held.tile([P, N], F32, name="scores")
-        nc.scalar.dma_start(scores[:], attr.broadcast_to([P, N]))
         wa_cols = held.tile([P, BLOCKS], F32, name="wa_cols")
         ba_cols = held.tile([P, BLOCKS], F32, name="ba_cols")
         b1_cols = held.tile([P, BLOCKS], F32, name="b1_cols")
-        with nc.allow_non_contiguous_dma(reason="one float32 to a partition, 256 in all"):
-            nc.scalar.dma_start(wa_cols[:], wa.rearrange("(k p) o -> p (k o)", p=P))
-            nc.scalar.dma_start(ba_cols[:], ba.rearrange("(k p) o -> p (k o)", p=P))
         weights = held.tile([P, BLOCKS, C], BF16, name="weights")
+
+        with nc.allow_non_contiguous_dma(reason="one float32 to a partition, 256 in all"):
+            nc.sync.dma_start(wa_cols[:], wa.rearrange("(k p) o -> p (k o)", p=P))
+            nc.sync.dma_start(ba_cols[:], ba.rearrange("(k p) o -> p (k o)", p=P))
+        nc.sync.dma_start(nodes[0][:], x[0:P, :])
+        nc.sync.dma_start(scores[:], attr.broadcast_to([P, N]))
+        nc.sync.dma_start(offsets[:], offs)
+        nc.scalar.dma_start(nodes[1][:], x[P : 2 * P, :])
         nc.scalar.dma_start(weights[:], w1.rearrange("(k p) m -> p k m", p=P))
         with nc.allow_non_contiguous_dma(reason="one float32 to a partition, 256 in all"):
-            nc.sync.dma_start(b1_cols[:], b1.rearrange("(k p) o -> p (k o)", p=P))
+            nc.scalar.dma_start(b1_cols[:], b1.rearrange("(k p) o -> p (k o)", p=P))
 
         attract = []
         for k in range(BLOCKS):

@@ -29,14 +29,14 @@ def tile_topicpropagationmodel_kernel(tc, x, attr, wa, ba, w1, b1, offs, out):
 
         with nc.allow_non_contiguous_dma(reason="one float32 to a partition, 256 in all"):
             nc.sync.dma_start(wa_cols[:], wa.rearrange("(k p) o -> p (k o)", p=P))
-            nc.sync.dma_start(ba_cols[:], ba.rearrange("(k p) o -> p (k o)", p=P))
-        nc.sync.dma_start(nodes[0][:], x[0:P, :])
+            nc.scalar.dma_start(ba_cols[:], ba.rearrange("(k p) o -> p (k o)", p=P))
         nc.sync.dma_start(scores[:], attr.broadcast_to([P, N]))
+        nc.scalar.dma_start(nodes[0][:], x[0:P, :])
         nc.sync.dma_start(offsets[:], offs)
         nc.scalar.dma_start(nodes[1][:], x[P : 2 * P, :])
         nc.scalar.dma_start(weights[:], w1.rearrange("(k p) m -> p k m", p=P))
         with nc.allow_non_contiguous_dma(reason="one float32 to a partition, 256 in all"):
-            nc.scalar.dma_start(b1_cols[:], b1.rearrange("(k p) o -> p (k o)", p=P))
+            nc.sync.dma_start(b1_cols[:], b1.rearrange("(k p) o -> p (k o)", p=P))
 
         attract = []
         for k in range(BLOCKS):

@@ -6,6 +6,7 @@ U16 = mybir.dt.uint16
 ADD = mybir.AluOpType.add
 MULT = mybir.AluOpType.mult
 MAX = mybir.AluOpType.max
+IDENTITY = mybir.ActivationFunctionType.Identity
 
 P = 128
 C = 256
@@ -38,13 +39,18 @@ def tile_topicpropagationmodel_kernel(tc, x, attr, wa, ba, w1, b1, offs, out):
         with nc.allow_non_contiguous_dma(reason="one float32 to a partition, 256 in all"):
             nc.sync.dma_start(b1_cols[:], b1.rearrange("(k p) o -> p (k o)", p=P))
 
-        attract = []
-        for k in range(BLOCKS):
-            attract_k = held.tile([P, N], F32, name=f"attract{k}")
-            nc.vector.tensor_scalar(
-                attract_k[:], scores[:], wa_cols[:, k : k + 1], ba_cols[:, k : k + 1], MULT, ADD
-            )
-            attract.append(attract_k)
+        warm_in = held.tile([P, 1], F32, name="warm_in")
+        warm_out = held.tile([P, 1], F32, name="warm_out")
+        nc.vector.memset(warm_in[:], 0.0)
+        nc.scalar.activation(warm_out[:], warm_in[:], IDENTITY)
+
+        attract = [held.tile([P, N], F32, name=f"attract{k}") for k in range(BLOCKS)]
+        nc.vector.tensor_scalar(
+            attract[0][:], scores[:], wa_cols[:, 0:1], ba_cols[:, 0:1], MULT, ADD
+        )
+        nc.scalar.activation(
+            attract[1][:], scores[:], IDENTITY, bias=ba_cols[:, 1:2], scale=wa_cols[:, 1:2]
+        )
 
         product = [banks.tile([P, N], F32, name=f"product{m}") for m in range(BLOCKS)]
 
@@ -52,7 +58,10 @@ def tile_topicpropagationmodel_kernel(tc, x, attr, wa, ba, w1, b1, offs, out):
             u_f32 = held.tile([P, N], F32, name=f"u_f32_{k}")
             nc.vector.tensor_tensor(u_f32[:], nodes[k][:].indirect(offsets[:]), attract[k][:], ADD)
             u_bf16 = held.tile([P, N], BF16, name=f"u_bf16_{k}")
-            nc.vector.tensor_copy(u_bf16[:], u_f32[:])
+            if k < BLOCKS - 1:
+                nc.scalar.activation(u_bf16[:], u_f32[:], IDENTITY)
+            else:
+                nc.vector.tensor_copy(u_bf16[:], u_f32[:])
             for m in range(BLOCKS):
                 nc.tensor.matmul(
                     product[m][:],

@@ -6,7 +6,6 @@ U16 = mybir.dt.uint16
 ADD = mybir.AluOpType.add
 MULT = mybir.AluOpType.mult
 MAX = mybir.AluOpType.max
-IDENTITY = mybir.ActivationFunctionType.Identity
 
 P = 128
 C = 256
@@ -28,29 +27,24 @@ def tile_topicpropagationmodel_kernel(tc, x, attr, wa, ba, w1, b1, offs, out):
         b1_cols = held.tile([P, BLOCKS], F32, name="b1_cols")
         weights = held.tile([P, BLOCKS, C], BF16, name="weights")
 
-        with nc.allow_non_contiguous_dma(reason="one float32 to a partition, 256 in all"):
-            nc.sync.dma_start(wa_cols[:], wa.rearrange("(k p) o -> p (k o)", p=P))
-            nc.scalar.dma_start(ba_cols[:], ba.rearrange("(k p) o -> p (k o)", p=P))
+        x_blocks = x.rearrange("(p k) s -> k p s", k=BLOCKS)
+        nc.sync.dma_start(wa_cols[:], wa.rearrange("(p k) o -> p (k o)", k=BLOCKS))
+        nc.scalar.dma_start(ba_cols[:], ba.rearrange("(p k) o -> p (k o)", k=BLOCKS))
         nc.sync.dma_start(scores[:], attr.broadcast_to([P, N]))
-        nc.scalar.dma_start(nodes[0][:], x[0:P, :])
+        nc.scalar.dma_start(nodes[0][:], x_blocks[0, :, :])
         nc.sync.dma_start(offsets[:], offs)
-        nc.scalar.dma_start(nodes[1][:], x[P : 2 * P, :])
-        nc.scalar.dma_start(weights[:], w1.rearrange("(k p) m -> p k m", p=P))
+        nc.scalar.dma_start(nodes[1][:], x_blocks[1, :, :])
+        nc.scalar.dma_start(weights[:], w1.rearrange("(p k) m -> p k m", k=BLOCKS))
         with nc.allow_non_contiguous_dma(reason="one float32 to a partition, 256 in all"):
-            nc.sync.dma_start(b1_cols[:], b1.rearrange("(k p) o -> p (k o)", p=P))
+            nc.sync.dma_start(b1_cols[:], b1.rearrange("(m p) o -> p (m o)", p=P))
 
-        warm_in = held.tile([P, 1], F32, name="warm_in")
-        warm_out = held.tile([P, 1], F32, name="warm_out")
-        nc.vector.memset(warm_in[:], 0.0)
-        nc.scalar.activation(warm_out[:], warm_in[:], IDENTITY)
-
-        attract = [held.tile([P, N], F32, name=f"attract{k}") for k in range(BLOCKS)]
-        nc.vector.tensor_scalar(
-            attract[0][:], scores[:], wa_cols[:, 0:1], ba_cols[:, 0:1], MULT, ADD
-        )
-        nc.scalar.activation(
-            attract[1][:], scores[:], IDENTITY, bias=ba_cols[:, 1:2], scale=wa_cols[:, 1:2]
-        )
+        attract = []
+        for k in range(BLOCKS):
+            attract_k = held.tile([P, N], F32, name=f"attract{k}")
+            nc.vector.tensor_scalar(
+                attract_k[:], scores[:], wa_cols[:, k : k + 1], ba_cols[:, k : k + 1], MULT, ADD
+            )
+            attract.append(attract_k)
 
         product = [banks.tile([P, N], F32, name=f"product{m}") for m in range(BLOCKS)]
 
@@ -58,10 +52,7 @@ def tile_topicpropagationmodel_kernel(tc, x, attr, wa, ba, w1, b1, offs, out):
             u_f32 = held.tile([P, N], F32, name=f"u_f32_{k}")
             nc.vector.tensor_tensor(u_f32[:], nodes[k][:].indirect(offsets[:]), attract[k][:], ADD)
             u_bf16 = held.tile([P, N], BF16, name=f"u_bf16_{k}")
-            if k < BLOCKS - 1:
-                nc.scalar.activation(u_bf16[:], u_f32[:], IDENTITY)
-            else:
-                nc.vector.tensor_copy(u_bf16[:], u_f32[:])
+            nc.vector.tensor_copy(u_bf16[:], u_f32[:])
             for m in range(BLOCKS):
                 nc.tensor.matmul(
                     product[m][:],

@@ -25,7 +25,7 @@ def tile_topicpropagationmodel_kernel(tc, x, attr, wa, ba, w1, b1, offs, out):
         wa_cols = held.tile([P, BLOCKS], F32, name="wa_cols")
         ba_cols = held.tile([P, BLOCKS], F32, name="ba_cols")
         b1_cols = held.tile([P, BLOCKS], F32, name="b1_cols")
-        weights = held.tile([P, BLOCKS, C], BF16, name="weights")
+        weights = held.tile([P, BLOCKS, P, BLOCKS], BF16, name="weights")
 
         x_blocks = x.rearrange("(p k) s -> k p s", k=BLOCKS)
         nc.sync.dma_start(wa_cols[:], wa.rearrange("(p k) o -> p (k o)", k=BLOCKS))
@@ -34,9 +34,8 @@ def tile_topicpropagationmodel_kernel(tc, x, attr, wa, ba, w1, b1, offs, out):
         nc.scalar.dma_start(nodes[0][:], x_blocks[0, :, :])
         nc.sync.dma_start(offsets[:], offs)
         nc.scalar.dma_start(nodes[1][:], x_blocks[1, :, :])
-        nc.scalar.dma_start(weights[:], w1.rearrange("(p k) m -> p k m", k=BLOCKS))
-        with nc.allow_non_contiguous_dma(reason="one float32 to a partition, 256 in all"):
-            nc.sync.dma_start(b1_cols[:], b1.rearrange("(m p) o -> p (m o)", p=P))
+        nc.scalar.dma_start(weights[:], w1.rearrange("(p k) (q m) -> p k q m", k=BLOCKS, m=BLOCKS))
+        nc.sync.dma_start(b1_cols[:], b1.rearrange("(p m) o -> p (m o)", m=BLOCKS))
 
         attract = []
         for k in range(BLOCKS):
@@ -56,13 +55,15 @@ def tile_topicpropagationmodel_kernel(tc, x, attr, wa, ba, w1, b1, offs, out):
             for m in range(BLOCKS):
                 nc.tensor.matmul(
                     product[m][:],
-                    weights[:, k, m * P : (m + 1) * P],
+                    weights[:, k, :, m],
                     u_bf16[:],
                     start=(k == 0),
                     stop=(k == BLOCKS - 1),
                 )
 
+        result = held.tile([P, BLOCKS, N], F32, name="result")
         for m in range(BLOCKS):
-            result = held.tile([P, N], F32, name=f"result{m}")
-            nc.vector.tensor_scalar(result[:], product[m][:], b1_cols[:, m : m + 1], 0.0, ADD, MAX)
-            nc.sync.dma_start(out[m * P : (m + 1) * P, :], result[:])
+            nc.vector.tensor_scalar(
+                result[:, m, :], product[m][:], b1_cols[:, m : m + 1], 0.0, ADD, MAX
+            )
+        nc.sync.dma_start(out.rearrange("(p m) j -> p m j", m=BLOCKS), result[:])

@@ -61,9 +61,8 @@ def tile_topicpropagationmodel_kernel(tc, x, attr, wa, ba, w1, b1, offs, out):
                     stop=(k == BLOCKS - 1),
                 )
 
-        result = held.tile([P, BLOCKS, N], F32, name="result")
+        out_blocks = out.rearrange("(p m) j -> m p j", m=BLOCKS)
         for m in range(BLOCKS):
-            nc.vector.tensor_scalar(
-                result[:, m, :], product[m][:], b1_cols[:, m : m + 1], 0.0, ADD, MAX
-            )
-        nc.sync.dma_start(out.rearrange("(p m) j -> p m j", m=BLOCKS), result[:])
+            result = held.tile([P, N], F32, name=f"result{m}")
+            nc.vector.tensor_scalar(result[:], product[m][:], b1_cols[:, m : m + 1], 0.0, ADD, MAX)
+            nc.sync.dma_start(out_blocks[m, :, :], result[:])

@@ -6,6 +6,7 @@ U16 = mybir.dt.uint16
 ADD = mybir.AluOpType.add
 MULT = mybir.AluOpType.mult
 MAX = mybir.AluOpType.max
+IDENTITY = mybir.ActivationFunctionType.Identity
 
 P = 128
 C = 256
@@ -37,13 +38,14 @@ def tile_topicpropagationmodel_kernel(tc, x, attr, wa, ba, w1, b1, offs, out):
         nc.scalar.dma_start(weights[:], w1.rearrange("(p k) (q m) -> p k q m", k=BLOCKS, m=BLOCKS))
         nc.sync.dma_start(b1_cols[:], b1.rearrange("(p m) o -> p (m o)", m=BLOCKS))
 
-        attract = []
-        for k in range(BLOCKS):
-            attract_k = held.tile([P, N], F32, name=f"attract{k}")
-            nc.vector.tensor_scalar(
-                attract_k[:], scores[:], wa_cols[:, k : k + 1], ba_cols[:, k : k + 1], MULT, ADD
-            )
-            attract.append(attract_k)
+        zeros = held.tile([P, 1], F32, name="zeros")
+        nc.vector.memset(zeros[:], 0.0)
+        table_loader = held.tile([P, 1], F32, name="table_loader")
+        nc.scalar.activation(table_loader[:], zeros[:], IDENTITY)
+
+        attract = [held.tile([P, N], F32, name=f"attract{k}") for k in range(BLOCKS)]
+        nc.vector.tensor_scalar(attract[0][:], scores[:], wa_cols[:, 0:1], ba_cols[:, 0:1], MULT, ADD)
+        nc.scalar.activation(attract[1][:], scores[:], IDENTITY, bias=ba_cols[:, 1:2], scale=wa_cols[:, 1:2])
 
         product = [banks.tile([P, N], F32, name=f"product{m}") for m in range(BLOCKS)]
 
@@ -51,7 +53,10 @@ def tile_topicpropagationmodel_kernel(tc, x, attr, wa, ba, w1, b1, offs, out):
             u_f32 = held.tile([P, N], F32, name=f"u_f32_{k}")
             nc.vector.tensor_tensor(u_f32[:], nodes[k][:].indirect(offsets[:]), attract[k][:], ADD)
             u_bf16 = held.tile([P, N], BF16, name=f"u_bf16_{k}")
-            nc.vector.tensor_copy(u_bf16[:], u_f32[:])
+            if k == 0:
+                nc.scalar.copy(u_bf16[:], u_f32[:])
+            else:
+                nc.vector.tensor_copy(u_bf16[:], u_f32[:])
             for m in range(BLOCKS):
                 nc.tensor.matmul(
                     product[m][:],

@@ -22,16 +22,16 @@ def tile_topicpropagationmodel_kernel(tc, x, attr, wa, ba, w1, b1, offs, out):
     with tc.tile_pool(name="held", bufs=1) as held, tc.psum_pool(name="banks", bufs=1) as banks:
         offsets = held.tile([P, N // 16], U16, name="offsets")
         nodes = [held.tile([P, S], F32, name=f"nodes{k}") for k in range(BLOCKS)]
-        scores = held.tile([P, N], F32, name="scores")
+        scores_row = held.tile([1, N], F32, name="scores_row")
         wa_cols = held.tile([P, BLOCKS], F32, name="wa_cols")
         ba_cols = held.tile([P, BLOCKS], F32, name="ba_cols")
         b1_cols = held.tile([P, BLOCKS], F32, name="b1_cols")
         weights = held.tile([P, BLOCKS, P, BLOCKS], BF16, name="weights")
 
         x_blocks = x.rearrange("(p k) s -> k p s", k=BLOCKS)
-        nc.sync.dma_start(wa_cols[:], wa.rearrange("(p k) o -> p (k o)", k=BLOCKS))
+        nc.sync.dma_start(scores_row[:], attr)
         nc.scalar.dma_start(ba_cols[:], ba.rearrange("(p k) o -> p (k o)", k=BLOCKS))
-        nc.sync.dma_start(scores[:], attr.broadcast_to([P, N]))
+        nc.sync.dma_start(wa_cols[:], wa.rearrange("(p k) o -> p (k o)", k=BLOCKS))
         nc.scalar.dma_start(nodes[0][:], x_blocks[0, :, :])
         nc.sync.dma_start(offsets[:], offs)
         nc.scalar.dma_start(nodes[1][:], x_blocks[1, :, :])
@@ -42,6 +42,11 @@ def tile_topicpropagationmodel_kernel(tc, x, attr, wa, ba, w1, b1, offs, out):
         nc.vector.memset(zeros[:], 0.0)
         table_loader = held.tile([P, 1], F32, name="table_loader")
         nc.scalar.activation(table_loader[:], zeros[:], IDENTITY)
+
+        ones = held.tile([1, P], F32, name="ones")
+        nc.vector.memset(ones[:], 1.0)
+        scores = banks.tile([P, N], F32, name="scores")
+        nc.tensor.matmul(scores[:], ones[:], scores_row[:], start=True, stop=True)
 
         attract = [held.tile([P, N], F32, name=f"attract{k}") for k in range(BLOCKS)]
         nc.vector.tensor_scalar(attract[0][:], scores[:], wa_cols[:, 0:1], ba_cols[:, 0:1], MULT, ADD)

import concourse.mybir as mybir

F32 = mybir.dt.float32
BF16 = mybir.dt.bfloat16
U16 = mybir.dt.uint16
ADD = mybir.AluOpType.add
MULT = mybir.AluOpType.mult
MAX = mybir.AluOpType.max
IDENTITY = mybir.ActivationFunctionType.Identity

P = 128
C = 256
S = 256
N = 128
BLOCKS = C // P

FLOPS = 2 * C * C * N


def tile_topicpropagationmodel_kernel(tc, x, attr, wa, ba, w1, b1, offs, out):
    nc = tc.nc
    with tc.tile_pool(name="held", bufs=1) as held, tc.psum_pool(name="banks", bufs=1) as banks:
        offsets = held.tile([P, N // 16], U16, name="offsets")
        nodes = [held.tile([P, S], F32, name=f"nodes{k}") for k in range(BLOCKS)]
        scores_row = held.tile([1, N], F32, name="scores_row")
        wa_cols = held.tile([P, BLOCKS], F32, name="wa_cols")
        ba_cols = held.tile([P, BLOCKS], F32, name="ba_cols")
        b1_cols = held.tile([P, BLOCKS], F32, name="b1_cols")
        weights = held.tile([P, BLOCKS, P, BLOCKS], BF16, name="weights")

        x_blocks = x.rearrange("(p k) s -> k p s", k=BLOCKS)
        nc.sync.dma_start(scores_row[:], attr)
        nc.scalar.dma_start(ba_cols[:], ba.rearrange("(p k) o -> p (k o)", k=BLOCKS))
        nc.sync.dma_start(wa_cols[:], wa.rearrange("(p k) o -> p (k o)", k=BLOCKS))
        nc.scalar.dma_start(nodes[0][:], x_blocks[0, :, :])
        nc.sync.dma_start(offsets[:], offs)
        nc.scalar.dma_start(nodes[1][:], x_blocks[1, :, :])
        nc.scalar.dma_start(weights[:], w1.rearrange("(p k) (q m) -> p k q m", k=BLOCKS, m=BLOCKS))
        nc.sync.dma_start(b1_cols[:], b1.rearrange("(p m) o -> p (m o)", m=BLOCKS))

        zeros = held.tile([P, 1], F32, name="zeros")
        nc.vector.memset(zeros[:], 0.0)
        table_loader = held.tile([P, 1], F32, name="table_loader")
        nc.scalar.activation(table_loader[:], zeros[:], IDENTITY)

        ones = held.tile([1, P], F32, name="ones")
        nc.vector.memset(ones[:], 1.0)
        scores = banks.tile([P, N], F32, name="scores")
        nc.tensor.matmul(scores[:], ones[:], scores_row[:], start=True, stop=True)

        attract = [held.tile([P, N], F32, name=f"attract{k}") for k in range(BLOCKS)]
        nc.vector.tensor_scalar(attract[0][:], scores[:], wa_cols[:, 0:1], ba_cols[:, 0:1], MULT, ADD)
        nc.scalar.activation(attract[1][:], scores[:], IDENTITY, bias=ba_cols[:, 1:2], scale=wa_cols[:, 1:2])

        product = [banks.tile([P, N], F32, name=f"product{m}") for m in range(BLOCKS)]

        for k in range(BLOCKS):
            u_f32 = held.tile([P, N], F32, name=f"u_f32_{k}")
            nc.vector.tensor_tensor(u_f32[:], nodes[k][:].indirect(offsets[:]), attract[k][:], ADD)
            u_bf16 = held.tile([P, N], BF16, name=f"u_bf16_{k}")
            if k == 0:
                nc.scalar.copy(u_bf16[:], u_f32[:])
            else:
                nc.vector.tensor_copy(u_bf16[:], u_f32[:])
            for m in range(BLOCKS):
                nc.tensor.matmul(
                    product[m][:],
                    weights[:, k, :, m],
                    u_bf16[:],
                    start=(k == 0),
                    stop=(k == BLOCKS - 1),
                )

        out_blocks = out.rearrange("(p m) j -> m p j", m=BLOCKS)
        for m in range(BLOCKS):
            result = held.tile([P, N], F32, name=f"result{m}")
            nc.vector.tensor_scalar(result[:], product[m][:], b1_cols[:, m : m + 1], 0.0, ADD, MAX)
            nc.sync.dma_start(out_blocks[m, :, :], result[:])
